import numpy as np
import ml_dtypes


def mxq(x, axis, fmt="e4m3"):
    dtype, down = {"e4m3": (ml_dtypes.float8_e4m3fn, 7), "e5m2": (ml_dtypes.float8_e5m2, 14)}[fmt]
    v = np.moveaxis(np.asarray(x, np.float32).astype(ml_dtypes.bfloat16).astype(np.float64), axis, -1)
    blocks = v.reshape(v.shape[:-1] + (-1, 32))
    amax = np.abs(blocks).max(-1, keepdims=True)
    byte = np.maximum(np.where(amax > 0, np.frexp(amax)[1] - 1 + 127, 0) - down, 1)
    scale = np.exp2(byte - 127.0)
    codes = (blocks / scale).astype(np.float32).astype(dtype).astype(np.float64)
    return np.moveaxis((codes * scale).reshape(v.shape), -1, axis)


WIDE = False


def mx_kscale(k):
    if not WIDE:
        return np.ones(k)
    levels = np.array([18, -18])
    if k % 512:
        return np.exp2(np.random.permutation(np.resize(levels, k // 32))).repeat(32)
    a = np.empty((k // 512, 16))
    for p in range(k // 512):
        a[p, :8] = np.random.permutation(np.resize(levels, 8))
        for g in range(8):
            far = levels[np.abs(levels - a[p, g]) >= 10]
            a[p, g + 8] = far[np.random.randint(len(far))]
    return np.exp2(a.ravel()).repeat(32)


BF16 = ml_dtypes.bfloat16


def bf(x):
    return np.asarray(x, np.float32).astype(BF16)


def f64(x):
    return np.asarray(x).astype(np.float64)


B, N, H, F, M, C = 128, 4, 1024, 1024, 1024, 3
T = B * N
E = B * N * N


def sigmoid(v):
    return 1.0 / (1.0 + np.exp(-v))


def distances(p):
    rel = p[:, :, None, :] - p[:, None, :, :]
    sq = np.sum(rel * rel, axis=-1, keepdims=True)
    return np.where(sq > 0, np.sqrt(np.where(sq > 0, sq, 1.0)), 0.0)


def setup_inputs():
    s = mx_kscale(T).reshape(B, N)[:, :, None]
    u = mx_kscale(M)
    v = mx_kscale(F)
    w_nodes = np.random.standard_normal((2, H, F)) / np.sqrt(2 * H)
    w_dist = np.random.standard_normal((1, F)) * 0.3
    x0 = bf(np.random.standard_normal((B, N, H)))
    p0 = bf(np.random.standard_normal((B, N, C)))
    w1_0 = bf(np.concatenate([w_nodes.reshape(2 * H, F), w_dist], 0))
    be1 = bf(np.random.standard_normal(F) * 0.5)
    w2_0 = bf(np.random.standard_normal((F, M)) / np.sqrt(F))
    be2 = bf(np.random.standard_normal(M) * 0.5)
    g = bf(np.random.standard_normal((B, N, N, M)) * np.exp2(np.random.randint(-6, 1, (B, N, N, 1))) / s[:, :, None, :] * u)
    w1f = f64(w1_0)
    a_i = f64(x0) @ w1f[:H]
    a_j = f64(x0) @ w1f[H:2 * H]
    pre = a_i[:, :, None, :] + a_j[:, None, :, :] + distances(f64(p0)) * w1f[2 * H] + f64(be1)
    return {"node_state": bf(f64(x0) * s),
            "positions": bf(f64(p0) * s),
            "We1": bf(w1f / v),
            "be1": be1,
            "We2": bf(f64(w2_0) * v[:, None] / u),
            "be2": be2,
            "pre": np.asarray(pre, np.float32),
            "grad_out": g}


def reference(node_state, positions, We1, be1, We2, be2, pre, grad_out):
    x = f64(node_state).reshape(T, H)
    w1 = f64(We1)
    zf = f64(pre).reshape(E, F)
    dist = distances(f64(positions)).reshape(E, 1)
    sg = sigmoid(zf)
    g = f64(grad_out).reshape(E, M)
    dh = mxq(g, 1, "e5m2") @ mxq(f64(We2), 1, "e4m3").T
    dpre = dh * (sg * (1.0 + zf * (1.0 - sg)))
    d4 = dpre.reshape(B, N, N, F)
    da_i = np.sum(d4, axis=2).reshape(T, F)
    da_j = np.sum(d4, axis=1).reshape(T, F)
    d = np.concatenate([da_i, da_j], axis=1)
    wcat = np.concatenate([w1[:H], w1[H:2 * H]], axis=1)
    dx = mxq(d, 1, "e5m2") @ mxq(wcat, 1, "e4m3").T
    dw = mxq(x, 0, "e4m3").T @ mxq(d, 0, "e5m2")
    dw_dist = np.sum(dist * dpre, axis=0, keepdims=True)
    dw1 = np.concatenate([dw[:, :F], dw[:, F:], dw_dist], axis=0)
    return dx.reshape(B, N, H), dw1

@@ -1,0 +1,459 @@
+from contextlib import ExitStack
+
+import concourse.mybir as mybir
+from concourse.masks import make_identity
+
+B, NODES, H, F, M = 128, 4, 1024, 1024, 1024
+PAIRS = B * NODES * NODES
+FLOPS = 2 * PAIRS * M * F + 2 * 2 * B * NODES * 2 * F * H
+BYTES = 2 * (B * NODES * H + B * NODES * 3 + 2 * H * F + F * M + PAIRS * M) + 4 * (
+    PAIRS * F + B * NODES * H + (2 * H + 1) * F
+)
+
+F32 = mybir.dt.float32
+BF16 = mybir.dt.bfloat16
+U32 = mybir.dt.uint32
+U8 = mybir.dt.uint8
+E4M3 = mybir.dt.float8_e4m3fn_x4
+E5M2 = mybir.dt.float8_e5m2_x4
+ACT = mybir.ActivationFunctionType
+ALU = mybir.AluOpType
+AXIS = mybir.AxisListType
+
+P = 128
+BANK = 512
+CHUNKS = F // BANK
+TILES = PAIRS // P
+STEPS = TILES // 2
+GRAPHS = P // (NODES * NODES)
+SUM_COLS = 2 * GRAPHS * NODES
+SEL_COLS = SUM_COLS + 2
+
+
+def tile_graphmessagelayer_pa_v_kernel(
+    tc, node_state, positions, We1, be1, We2, be2, pre, grad_out, out_0, out_1
+):
+    nc = tc.nc
+    g_rows = grad_out.rearrange("b i j m -> (b i j) m")
+    pre_rows = pre.rearrange("b i j f -> (b i j) f")
+
+    with ExitStack() as ctx:
+        const = ctx.enter_context(tc.tile_pool(name="const", bufs=1))
+        work = ctx.enter_context(tc.tile_pool(name="work", bufs=1))
+        psum = ctx.enter_context(tc.psum_pool(name="psum", bufs=1))
+        ctx.enter_context(tc.manual_schedule())
+
+        def new_bank():
+            return psum.tile([P, BANK], F32, name="bank", tag="bank", bufs=6)
+
+        def copy(engine, out, in_):
+            if engine == "scalar":
+                nc.scalar.copy(out=out, in_=in_)
+            else:
+                nc.vector.tensor_copy(out=out, in_=in_)
+
+        loaded = {}
+        mx = {}
+
+        def load_g(s):
+            t = work.tile([P, 2, M], BF16, name="raw4", tag="raw4", bufs=5)
+            nc.sync.dma_start(out=t[:], in_=g_rows[2 * P * s : 2 * P * (s + 1), :].rearrange("(t q) m -> q t m", t=2))
+            loaded["g", s] = t
+
+        def load_we2(c, g):
+            t = work.tile([P, 4, BANK], BF16, name="raw4", tag="raw4", bufs=5)
+            rows = We2[BANK * c : BANK * (c + 1), BANK * g : BANK * (g + 1)]
+            nc.sync.dma_start(out=t[:], in_=rows.rearrange("(p t) m -> p t m", t=4))
+            loaded["we2", c, g] = t
+
+        def load_pre(i):
+            c, s = divmod(i, STEPS)
+            t = work.tile([P, 2, BANK], F32, name="pre_t", tag="pre_t", bufs=6)
+            rows = pre_rows[2 * P * s : 2 * P * (s + 1), BANK * c : BANK * (c + 1)]
+            nc.sync.dma_start(out=t[:], in_=rows.rearrange("(t q) f -> q t f", t=2))
+            loaded["pre", i] = t
+
+        def load_x():
+            t = work.tile([P, NODES, H], BF16, name="raw8", tag="raw8", bufs=3)
+            nc.sync.dma_start(out=t[:], in_=node_state)
+            loaded["x"] = t
+
+        def load_we1(half, hh):
+            t = work.tile([P, 4, F], BF16, name="raw8", tag="raw8", bufs=3)
+            r0 = H * half + BANK * hh
+            nc.sync.dma_start(out=t[:], in_=We1[r0 : r0 + BANK, :].rearrange("(t p) f -> p t f", t=4))
+            loaded["we1", half, hh] = t
+
+        def new_stage():
+            return work.tile([P, 2 * BANK], F32, name="stage", tag="stage", bufs=4, align_bytes=64)
+
+        def quantise(key, values, fmt):
+            codes = work.tile([P, BANK], U32, name="codes", tag="codes", bufs=30, align_bytes=64)
+            scales = work.tile([P, BANK], U8, name="scales", tag="scales", bufs=30, align_bytes=64)
+            nc.vector.quantize_mx(out=codes[:].bitcast(fmt), scales=scales[:], in_=values)
+            mx[key] = (codes, scales, fmt)
+
+        def matmul_mx(bank, lhs_key, lhs_block, rhs_key, start, stop):
+            l_codes, l_scales, l_fmt = mx[lhs_key]
+            r_codes, r_scales, r_fmt = mx[rhs_key]
+            cols = slice(P * lhs_block, P * (lhs_block + 1))
+            nc.tensor.matmul_mx(
+                out=bank[:],
+                lhsT=l_codes[:, cols].bitcast(l_fmt),
+                lhsT_scale=l_scales[:, cols],
+                rhs=r_codes[:].bitcast(r_fmt),
+                rhs_scale=r_scales[:],
+                start=start,
+                stop=stop,
+            )
+
+        def every_second_word(words, first, v):
+            return words[:, first + v : first + 2 * P : 2]
+
+        def turn(key):
+            banks = []
+            for j in range(2):
+                bank = new_bank()
+                for k in range(4):
+                    a, v = divmod(k, 2)
+                    if key[0] == "g":
+                        words = loaded[key][:].rearrange("p t m -> p (t m)").bitcast(F32)
+                        src = every_second_word(words, 512 * j + 256 * a, v)
+                    elif key[0] == "we2":
+                        words = loaded[key][:].rearrange("p t m -> p (t m)").bitcast(F32)
+                        src = every_second_word(words, 256 * (2 * a + j), v)
+                    elif key[0] == "we1":
+                        words = loaded[key[:3]][:].rearrange("p t m -> p (t m)").bitcast(F32)
+                        src = every_second_word(words, 512 * (2 * j + a) + 256 * key[3], v)
+                    else:
+                        words = d_feat[key[1]][:].bitcast(F32)
+                        src = every_second_word(words, 256 * (NODES * key[2] + k), j)
+                    nc.tensor.transpose(bank[:, P * k : P * (k + 1)], src, ident[:])
+                banks.append(bank)
+            return {"key": key, "banks": banks, "stage": new_stage()}
+
+        def empty(job, j, engine):
+            bank, stage = job["banks"][j], job["stage"]
+            if job["key"][0] == "d_tok":
+                out = stage[:, BANK * j : BANK * (j + 1)].bitcast(BF16).rearrange("p (k n) -> p k n", n=NODES)
+                copy(engine, out, bank[:].bitcast(BF16).rearrange("p (n k) -> p k n", n=NODES))
+            else:
+                out = stage[:, BANK * j : BANK * (j + 1)].rearrange("p (a r v) -> p a r v", a=2, v=2)
+                copy(engine, out, bank[:].rearrange("p (a v r) -> p a r v", a=2, v=2))
+
+        def quantise_job(job):
+            fmt = E5M2 if job["key"][0] in ("g", "d_tok") else E4M3
+            quantise(job["key"], job["stage"][:].bitcast(BF16), fmt)
+
+        def interleave_x(hh):
+            stage = new_stage()
+            dst = stage[:].bitcast(BF16).rearrange("p (c i n) -> p c n i", i=4, n=NODES)
+            src = loaded["x"][:, :, BANK * hh : BANK * (hh + 1)].rearrange("p n (c i) -> p c n i", i=4)
+            nc.vector.tensor_copy(out=dst, in_=src)
+            return {"key": ("x", hh), "stage": stage}
+
+        acts = {}
+
+        def activations(i, a):
+            src = loaded["pre", i][:, a, :].rearrange("q (w u e) -> q u w e", u=2, e=2)
+            if a == 0:
+                acts[i, "th"] = work.tile([P, 2, BANK], F32, name="th", tag="th", bufs=3)
+            th = acts[i, "th"]
+            sn = work.tile([P, BANK], F32, name="sn", tag="sn", bufs=5)
+            nc.scalar.activation(out=sn[:].rearrange("q (u w e) -> q u w e", u=2, e=2), in_=src, func=ACT.Silu, scale=-1.0)
+            nc.scalar.activation(out=th[:, a, :].rearrange("q (u w e) -> q u w e", u=2, e=2), in_=src, func=ACT.Tanh, scale=0.5)
+            acts[i, a] = sn
+
+        dh_banks = {}
+
+        def dh_matmuls(i):
+            c, s = divmod(i, STEPS)
+            for a in range(2):
+                bank = new_bank()
+                for g in range(2):
+                    matmul_mx(bank, ("g", s), 2 * a + g, ("we2", c, g), g == 0, g == 1)
+                dh_banks[i, a] = bank
+
+        dpre = {}
+
+        def elementwise(i):
+            part = work.tile([P, 2, 2, BANK // 2], F32, name="part", tag="part", bufs=2)
+            for a in range(2):
+                nc.vector.scalar_tensor_tensor(
+                    out=part[:, :, a, :],
+                    in0=acts[i, a][:].rearrange("q (w e) -> q e w", e=2),
+                    scalar=1.0,
+                    in1=dh_banks[i, a][:].rearrange("q (e w) -> q e w", e=2),
+                    op0=ALU.subtract,
+                    op1=ALU.mult,
+                )
+            return part
+
+        def finish_elementwise(i, part):
+            t = work.tile([P, 2, BANK], F32, name="dpre_t", tag="dpre_t", bufs=3)
+            nc.vector.scalar_tensor_tensor(
+                out=t[:],
+                in0=acts[i, "th"][:].rearrange("q a (w e) -> q e (a w)", e=2),
+                scalar=1.0,
+                in1=part[:].rearrange("q e a w -> q e (a w)"),
+                op0=ALU.add,
+                op1=ALU.mult,
+            )
+            dpre[i] = t
+
+        def sum_window(i, a):
+            return sum_banks[a][:].rearrange("p (t k) -> p t k", t=4)[:, :, 2 * i : 2 * i + SEL_COLS]
+
+        def node_sums(i):
+            s = i % STEPS
+            for a in range(2):
+                for t in range(4):
+                    u, e = divmod(t, 2)
+                    first_col = 2 * P * a + P * u
+                    nc.tensor.matmul(
+                        sum_window(i, a)[:, t, :],
+                        lhsT=dpre[i][:, e, first_col : first_col + P],
+                        rhs=sel[:, 2 * s + a, :],
+                        start=True,
+                        stop=True,
+                    )
+
+        d_feat = {}
+
+        def empty_sums(i):
+            c, s = divmod(i, STEPS)
+            if s == 0:
+                d_feat[c] = work.tile([P, 2 * B * NODES * 4], BF16, name="d_feat", tag="d_feat", bufs=2, align_bytes=64)
+            for a in range(2):
+                tl = 2 * s + a
+                sums = sum_window(i, a)[:, :, 2:].rearrange("p t (n b) -> p n b t", b=GRAPHS)
+                out = d_feat[c][:].rearrange("p (n b t) -> p n b t", b=B, t=4)[:, :, GRAPHS * tl : GRAPHS * (tl + 1), :]
+                nc.vector.tensor_copy(out=out, in_=sums)
+
+        def quantise_d_feat(c, half):
+            width = B * NODES * 4
+            quantise(("d_feat", c, half), d_feat[c][:, width * half : width * (half + 1)], E5M2)
+
+        def new_result():
+            return work.tile([P, BANK], F32, name="result", tag="result", bufs=7)
+
+        def dw_block(c, k, engine):
+            half, hb = divmod(k, H // P)
+            bank = new_bank()
+            matmul_mx(bank, ("x", hb // 4), hb % 4, ("d_tok", c, half), True, True)
+
+            def finish():
+                res = new_result()
+                copy(
+                    engine,
+                    res[:].rearrange("h (w u e) -> h w u e", u=2, e=2),
+                    bank[:].rearrange("h (u w e) -> h w u e", u=2, e=2),
+                )
+                r0 = H * half + P * hb
+                nc.sync.dma_start(out=out_1[r0 : r0 + P, BANK * c : BANK * (c + 1)], in_=res[:])
+
+            return finish
+
+        def dx_passes(bank, n, hh, c):
+            for half in range(2):
+                matmul_mx(
+                    bank, ("d_feat", c, half), n, ("we1", half, hh, c), c == 0 and half == 0, c == 1 and half == 1
+                )
+
+        def dx_finish(bank, n, hh, engine):
+            res = new_result()
+            copy(engine, res[:], bank[:])
+            nc.sync.dma_start(out=out_0[:, n, BANK * hh : BANK * (hh + 1)], in_=res[:])
+
+        load_we2(0, 0)
+        load_g(0)
+        load_we2(0, 1)
+        load_pre(0)
+        pos = const.tile([P, NODES, 3], BF16, name="pos")
+        nc.sync.dma_start(out=pos[:], in_=positions)
+        load_g(1)
+        load_pre(1)
+        load_g(2)
+        for i in range(2, 5):
+            load_pre(i)
+
+        ident = const.tile([P, P], F32, name="ident")
+        make_identity(nc, ident[:])
+        warm = const.tile([P, 1], F32, name="warm")
+        nc.scalar.activation(out=warm[:], in_=ident[:, 0:1], func=ACT.Silu, scale=-1.0)
+
+        sel = const.tile([P, TILES, SEL_COLS], F32, name="sel")
+        pick = const.tile([P, 2, NODES, GRAPHS], F32, name="pick")
+        in_tile = const.tile([P, TILES], F32, name="in_tile")
+        in_place = const.tile([P, GRAPHS], F32, name="in_place")
+        dist_parts = const.tile([P, 2, 4, CHUNKS], F32, name="dist_parts")
+        sum_banks = [psum.tile([P, BANK], F32, name="sums", tag="sums", bufs=2) for a in range(2)]
+        dist_cols = const.tile([P, 4, P], F32, name="dist_cols")
+        nc.vector.memset(sel[:], 0.0)
+        nc.vector.memset(dist_cols[:], 0.0)
+        pair_view = ident[:].rearrange("q (b i j) -> q b i j", i=NODES, j=NODES)
+        nc.vector.tensor_reduce(out=pick[:, 0], in_=pair_view.rearrange("q b i j -> q i b j"), axis=AXIS.X, op=ALU.add)
+        nc.vector.tensor_reduce(out=pick[:, 1], in_=pair_view.rearrange("q b i j -> q j b i"), axis=AXIS.X, op=ALU.add)
+        graph_view = ident[:].rearrange("b (t g) -> b t g", g=GRAPHS)
+        nc.vector.tensor_reduce(out=in_tile[:], in_=graph_view, axis=AXIS.X, op=ALU.add)
+        nc.vector.tensor_reduce(out=in_place[:], in_=graph_view.rearrange("b t g -> b g t"), axis=AXIS.X, op=ALU.add)
+        nc.vector.tensor_scalar(
+            out=sel[:, :, 2:],
+            in0=pick[:].rearrange("q h n g -> q (h n g)").unsqueeze(1).to_broadcast([P, TILES, SUM_COLS]),
+            scalar1=-0.5,
+            scalar2=None,
+            op0=ALU.mult,
+        )
+
+        half_power = const.tile([P, NODES * NODES], F32, name="half_power")
+        rel = const.tile([P, NODES, NODES, 3], F32, name="rel")
+        rel_sq = const.tile([P, NODES * NODES, 3], F32, name="rel_sq")
+        sq_xy = const.tile([P, NODES * NODES], F32, name="sq_xy")
+        sq = const.tile([P, NODES * NODES], F32, name="sq")
+        dist = const.tile([P, NODES * NODES], F32, name="dist")
+        dist_spread = const.tile([P, GRAPHS, NODES * NODES], F32, name="dist_spread")
+        nc.gpsimd.memset(half_power[:], 0.5)
+        nc.gpsimd.tensor_tensor(
+            out=rel[:],
+            in0=pos[:].unsqueeze(2).to_broadcast([P, NODES, NODES, 3]),
+            in1=pos[:].unsqueeze(1).to_broadcast([P, NODES, NODES, 3]),
+            op=ALU.subtract,
+        )
+        rel_flat = rel[:].rearrange("b i j c -> b (i j) c")
+        nc.gpsimd.tensor_tensor(out=rel_sq[:], in0=rel_flat, in1=rel_flat, op=ALU.mult)
+        nc.gpsimd.tensor_tensor(out=sq_xy[:], in0=rel_sq[:, :, 0], in1=rel_sq[:, :, 1], op=ALU.add)
+        nc.gpsimd.tensor_tensor(out=sq[:], in0=sq_xy[:], in1=rel_sq[:, :, 2], op=ALU.add)
+        nc.gpsimd.tensor_tensor(out=dist[:], in0=sq[:], in1=half_power[:], op=ALU.pow)
+        nc.gpsimd.tensor_tensor(
+            out=dist_spread[:],
+            in0=dist[:].unsqueeze(1).to_broadcast([P, GRAPHS, NODES * NODES]),
+            in1=in_place[:].unsqueeze(2).to_broadcast([P, GRAPHS, NODES * NODES]),
+            op=ALU.mult,
+        )
+
+        first = []
+        for key in (("we2", 0, 0), ("g", 0), ("we2", 0, 1)):
+            job = turn(key)
+            empty(job, 0, "vector")
+            empty(job, 1, "scalar")
+            if first:
+                quantise_job(first[-1])
+            first.append(job)
+        job = turn(("g", 1))
+        empty(job, 0, "vector")
+        quantise_job(first[-1])
+        empty(job, 1, "vector")
+        activations(0, 0)
+        activations(0, 1)
+        waiting = [job]
+
+        we1_order = [(half, hh) for hh in range(2) for half in range(2)]
+        we1_jobs = [("we1", half, hh, c) for half, hh in we1_order for c in range(CHUNKS)]
+        turns = {i: [("g", i + 2)] for i in range(STEPS - 2)}
+        turns[6] = [("we2", 1, 0), ("we2", 1, 1)]
+        turns[10] = [("d_tok", 0, 0)]
+        turns[11] = [("d_tok", 0, 1)]
+        for i, key in zip((7, 8, 9, 12, 13, 14, 15, 16), we1_jobs):
+            turns[i] = [key]
+        dw_left = list(range(2 * H // P))
+        last = CHUNKS * STEPS
+
+        for i in range(last + 1):
+            if i + 3 < STEPS:
+                load_g(i + 3)
+            if i in (3, 4):
+                load_we2(1, i - 3)
+            if i + 5 < last:
+                load_pre(i + 5)
+            if i == 1:
+                load_x()
+            if i in (2, 5, 10, 13):
+                load_we1(*we1_order[(2, 5, 10, 13).index(i)])
+
+            if i == 1:
+                nc.vector.tensor_scalar(
+                    out=sel[:, :, 0], in0=dist_bank[:, :TILES], scalar1=-0.5, scalar2=None, op0=ALU.mult
+                )
+            for job in waiting:
+                quantise_job(job)
+            if i >= 1:
+                finish_elementwise(i - 1, part)
+            if i >= 2:
+                empty_sums(i - 2)
+            if i in (10, 11):
+                quantise_d_feat(0, i - 10)
+            waiting = [turn(key) for key in turns[i]]
+            if i + 1 < last:
+                activations(i + 1, 0)
+            for job in waiting:
+                empty(job, 0, "scalar")
+                empty(job, 1, "scalar")
+            if i + 1 < last:
+                activations(i + 1, 1)
+            if i < last:
+                dh_matmuls(i)
+            finishes = []
+            if i >= 11:
+                for k in dw_left[:3]:
+                    finishes.append(dw_block(0, k, "vector" if k % 4 == 3 else "scalar"))
+                dw_left = dw_left[3:]
+            if i < last:
+                part = elementwise(i)
+            if i in (8, 9):
+                waiting.append(interleave_x(i - 8))
+            for finish in finishes:
+                finish()
+            if i == 0:
+                dist_bank = new_bank()
+                nc.tensor.matmul(
+                    dist_bank[:, :TILES],
+                    lhsT=dist_spread[:].rearrange("b g k -> b (g k)"),
+                    rhs=in_tile[:],
+                    start=True,
+                    stop=True,
+                )
+            elif i < last:
+                node_sums(i - 1)
+
+        open_banks = []
+        for n in range(2):
+            bank = new_bank()
+            dx_passes(bank, n, 0, 0)
+            open_banks.append(bank)
+        node_sums(last - 1)
+        empty_sums(last - 1)
+        tok = [turn(("d_tok", 1, half)) for half in range(2)]
+        quantise_d_feat(1, 0)
+        quantise_d_feat(1, 1)
+        empty(tok[0], 0, "scalar")
+        empty(tok[0], 1, "vector")
+        empty(tok[1], 0, "scalar")
+        quantise_job(waiting[0])
+        quantise_job(tok[0])
+        empty(tok[1], 1, "scalar")
+        for a in range(2):
+            kept = sum_banks[a][:].rearrange("p (t k) -> p t k", t=4)[:, :, 0 : 2 * last : 2]
+            nc.vector.tensor_reduce(
+                out=dist_parts[:, a], in_=kept.rearrange("p t (c k) -> p t c k", c=CHUNKS), axis=AXIS.X, op=ALU.add
+            )
+        nc.vector.tensor_tensor(out=dist_cols[:, :, :CHUNKS], in0=dist_parts[:, 0], in1=dist_parts[:, 1], op=ALU.add)
+        for n in range(NODES):
+            if n >= 2:
+                open_banks.append(new_bank())
+                dx_passes(open_banks[n], n, 0, 0)
+            dx_passes(open_banks[n], n, 0, 1)
+            dx_finish(open_banks[n], n, 0, "vector")
+        quantise_job(tok[1])
+        row_bank = sum_banks[0]
+        for t in range(4):
+            nc.tensor.transpose(row_bank[:, t : BANK : 4], dist_cols[:, t, :], ident[:])
+        row = new_result()
+        nc.scalar.copy(out=row[:32, :], in_=row_bank[:32, :])
+        nc.sync.dma_start(out=out_1[2 * H : 2 * H + 1, :].rearrange("o (c f) -> (o c) f", c=CHUNKS), in_=row[:CHUNKS, :])
+        for n in range(NODES):
+            for k in range(4 * n, 4 * n + 4):
+                dw_block(1, k, "vector" if k % 2 else "scalar")()
+            bank = new_bank()
+            dx_passes(bank, n, 1, 0)
+            dx_passes(bank, n, 1, 1)
+            dx_finish(bank, n, 1, "vector" if n % 2 else "scalar")

@@ -137,6 +137,9 @@ def tile_graphmessagelayer_pa_v_kernel(
             if job["key"][0] == "d_tok":
                 out = stage[:, BANK * j : BANK * (j + 1)].bitcast(BF16).rearrange("p (k n) -> p k n", n=NODES)
                 copy(engine, out, bank[:].bitcast(BF16).rearrange("p (n k) -> p k n", n=NODES))
+            elif job["key"][0] == "we2":
+                out = stage[:, BANK * j : BANK * (j + 1)].rearrange("p (r a v) -> p r a v", a=2, v=2)
+                copy(engine, out, bank[:].rearrange("p (a v r) -> p r a v", a=2, v=2))
             else:
                 out = stage[:, BANK * j : BANK * (j + 1)].rearrange("p (a r v) -> p a r v", a=2, v=2)
                 copy(engine, out, bank[:].rearrange("p (a v r) -> p a r v", a=2, v=2))
@@ -154,15 +157,11 @@ def tile_graphmessagelayer_pa_v_kernel(
 
         acts = {}
 
-        def activations(i, a):
-            src = loaded["pre", i][:, a, :].rearrange("q (w u e) -> q u w e", u=2, e=2)
-            if a == 0:
-                acts[i, "th"] = work.tile([P, 2, BANK], F32, name="th", tag="th", bufs=3)
-            th = acts[i, "th"]
-            sn = work.tile([P, BANK], F32, name="sn", tag="sn", bufs=5)
-            nc.scalar.activation(out=sn[:].rearrange("q (u w e) -> q u w e", u=2, e=2), in_=src, func=ACT.Silu, scale=-1.0)
-            nc.scalar.activation(out=th[:, a, :].rearrange("q (u w e) -> q u w e", u=2, e=2), in_=src, func=ACT.Tanh, scale=0.5)
-            acts[i, a] = sn
+        def activation(i, func, scale):
+            t = work.tile([P, 2, BANK], F32, name="act_t", tag="act_t", bufs=5)
+            src = loaded["pre", i][:].rearrange("q a (w e) -> q e (a w)", e=2)
+            nc.scalar.activation(out=t[:], in_=src, func=func, scale=scale)
+            acts[i, func] = t
 
         dh_banks = {}
 
@@ -181,7 +180,7 @@ def tile_graphmessagelayer_pa_v_kernel(
             for a in range(2):
                 nc.vector.scalar_tensor_tensor(
                     out=part[:, :, a, :],
-                    in0=acts[i, a][:].rearrange("q (w e) -> q e w", e=2),
+                    in0=acts[i, ACT.Silu][:, :, BANK // 2 * a : BANK // 2 * (a + 1)],
                     scalar=1.0,
                     in1=dh_banks[i, a][:].rearrange("q (e w) -> q e w", e=2),
                     op0=ALU.subtract,
@@ -193,9 +192,9 @@ def tile_graphmessagelayer_pa_v_kernel(
             t = work.tile([P, 2, BANK], F32, name="dpre_t", tag="dpre_t", bufs=3)
             nc.vector.scalar_tensor_tensor(
                 out=t[:],
-                in0=acts[i, "th"][:].rearrange("q a (w e) -> q e (a w)", e=2),
+                in0=acts[i, ACT.Tanh][:].rearrange("q e (w u) -> q u (e w)", u=2),
                 scalar=1.0,
-                in1=part[:].rearrange("q e a w -> q e (a w)"),
+                in1=part[:].rearrange("q e a (w u) -> q u (e a w)", u=2),
                 op0=ALU.add,
                 op1=ALU.mult,
             )
@@ -209,10 +208,10 @@ def tile_graphmessagelayer_pa_v_kernel(
             for a in range(2):
                 for t in range(4):
                     u, e = divmod(t, 2)
-                    first_col = 2 * P * a + P * u
+                    first_col = 2 * P * e + P * a
                     nc.tensor.matmul(
                         sum_window(i, a)[:, t, :],
-                        lhsT=dpre[i][:, e, first_col : first_col + P],
+                        lhsT=dpre[i][:, u, first_col : first_col + P],
                         rhs=sel[:, 2 * s + a, :],
                         start=True,
                         stop=True,
@@ -234,7 +233,12 @@ def tile_graphmessagelayer_pa_v_kernel(
             width = B * NODES * 4
             quantise(("d_feat", c, half), d_feat[c][:, width * half : width * (half + 1)], E5M2)
 
+        results_made = []
+
         def new_result():
+            results_made.append(None)
+            if len(results_made) > 10 and len(results_made) % 2:
+                return work.tile([P, BANK], F32, name="pre_t", tag="pre_t", bufs=6)
             return work.tile([P, BANK], F32, name="result", tag="result", bufs=7)
 
         def dw_block(c, k, engine):
@@ -265,17 +269,15 @@ def tile_graphmessagelayer_pa_v_kernel(
             copy(engine, res[:], bank[:])
             nc.sync.dma_start(out=out_0[:, n, BANK * hh : BANK * (hh + 1)], in_=res[:])
 
+        pos = const.tile([P, NODES, 3], BF16, name="pos")
+        nc.scalar.dma_start(out=pos[:], in_=positions)
         load_we2(0, 0)
         load_g(0)
         load_we2(0, 1)
-        load_pre(0)
-        pos = const.tile([P, NODES, 3], BF16, name="pos")
-        nc.sync.dma_start(out=pos[:], in_=positions)
         load_g(1)
-        load_pre(1)
+        load_pre(0)
         load_g(2)
-        for i in range(2, 5):
-            load_pre(i)
+        load_pre(1)
 
         ident = const.tile([P, P], F32, name="ident")
         make_identity(nc, ident[:])
@@ -343,8 +345,8 @@ def tile_graphmessagelayer_pa_v_kernel(
         empty(job, 0, "vector")
         quantise_job(first[-1])
         empty(job, 1, "vector")
-        activations(0, 0)
-        activations(0, 1)
+        activation(0, ACT.Silu, -1.0)
+        activation(0, ACT.Tanh, 0.5)
         waiting = [job]
 
         we1_order = [(half, hh) for hh in range(2) for half in range(2)]
@@ -353,54 +355,54 @@ def tile_graphmessagelayer_pa_v_kernel(
         turns[6] = [("we2", 1, 0), ("we2", 1, 1)]
         turns[10] = [("d_tok", 0, 0)]
         turns[11] = [("d_tok", 0, 1)]
-        for i, key in zip((7, 8, 9, 12, 13, 14, 15, 16), we1_jobs):
+        for i, key in zip([k for k in range(7, 16) if k not in turns], we1_jobs):
             turns[i] = [key]
         dw_left = list(range(2 * H // P))
         last = CHUNKS * STEPS
+        we1_steps = (4, 6, 10, 11)
 
-        for i in range(last + 1):
+        for i in range(last):
             if i + 3 < STEPS:
                 load_g(i + 3)
             if i in (3, 4):
                 load_we2(1, i - 3)
-            if i + 5 < last:
-                load_pre(i + 5)
-            if i == 1:
+            for k in range(i + 2, min(i + 2 + 4, last)):
+                if ("pre", k) not in loaded and (k <= 2 * i + 2):
+                    load_pre(k)
+            if i == 2:
                 load_x()
-            if i in (2, 5, 10, 13):
-                load_we1(*we1_order[(2, 5, 10, 13).index(i)])
+            if i in we1_steps:
+                load_we1(*we1_order[we1_steps.index(i)])
 
             if i == 1:
                 nc.vector.tensor_scalar(
                     out=sel[:, :, 0], in0=dist_bank[:, :TILES], scalar1=-0.5, scalar2=None, op0=ALU.mult
                 )
-            for job in waiting:
-                quantise_job(job)
-            if i >= 1:
-                finish_elementwise(i - 1, part)
             if i >= 2:
                 empty_sums(i - 2)
+            if i >= 1:
+                finish_elementwise(i - 1, part)
+            for job in waiting:
+                quantise_job(job)
             if i in (10, 11):
                 quantise_d_feat(0, i - 10)
             waiting = [turn(key) for key in turns[i]]
             if i + 1 < last:
-                activations(i + 1, 0)
+                activation(i + 1, ACT.Silu, -1.0)
             for job in waiting:
                 empty(job, 0, "scalar")
                 empty(job, 1, "scalar")
             if i + 1 < last:
-                activations(i + 1, 1)
-            if i < last:
-                dh_matmuls(i)
+                activation(i + 1, ACT.Tanh, 0.5)
+            dh_matmuls(i)
             finishes = []
             if i >= 11:
-                for k in dw_left[:3]:
-                    finishes.append(dw_block(0, k, "vector" if k % 4 == 3 else "scalar"))
-                dw_left = dw_left[3:]
-            if i < last:
-                part = elementwise(i)
-            if i in (8, 9):
-                waiting.append(interleave_x(i - 8))
+                for k in dw_left[:2]:
+                    finishes.append(dw_block(0, k, "scalar"))
+                dw_left = dw_left[2:]
+            part = elementwise(i)
+            if i in (3, 5):
+                waiting.append(interleave_x((3, 5).index(i)))
             for finish in finishes:
                 finish()
             if i == 0:
@@ -412,15 +414,26 @@ def tile_graphmessagelayer_pa_v_kernel(
                     start=True,
                     stop=True,
                 )
-            elif i < last:
+            else:
                 node_sums(i - 1)
 
+        empty_sums(last - 2)
+        finish_elementwise(last - 1, part)
+        for job in waiting:
+            quantise_job(job)
+        final_we1 = turn(we1_jobs[-1])
+        empty(final_we1, 0, "scalar")
+        empty(final_we1, 1, "scalar")
+        for k in dw_left[:6]:
+            dw_block(0, k, "scalar")()
+        node_sums(last - 1)
+        for k in dw_left[6:]:
+            dw_block(0, k, "scalar")()
         open_banks = []
         for n in range(2):
             bank = new_bank()
             dx_passes(bank, n, 0, 0)
             open_banks.append(bank)
-        node_sums(last - 1)
         empty_sums(last - 1)
         tok = [turn(("d_tok", 1, half)) for half in range(2)]
         quantise_d_feat(1, 0)
@@ -428,32 +441,38 @@ def tile_graphmessagelayer_pa_v_kernel(
         empty(tok[0], 0, "scalar")
         empty(tok[0], 1, "vector")
         empty(tok[1], 0, "scalar")
-        quantise_job(waiting[0])
         quantise_job(tok[0])
-        empty(tok[1], 1, "scalar")
+        for n in range(2):
+            dx_passes(open_banks[n], n, 0, 1)
+            dx_finish(open_banks[n], n, 0, "scalar")
+        empty(tok[1], 1, "vector")
+        for k in range(0, 3):
+            dw_block(1, k, "scalar")()
+        quantise_job(tok[1])
+        quantise_job(final_we1)
         for a in range(2):
             kept = sum_banks[a][:].rearrange("p (t k) -> p t k", t=4)[:, :, 0 : 2 * last : 2]
             nc.vector.tensor_reduce(
                 out=dist_parts[:, a], in_=kept.rearrange("p t (c k) -> p t c k", c=CHUNKS), axis=AXIS.X, op=ALU.add
             )
+        for k in range(3, 6):
+            dw_block(1, k, "scalar" if k % 2 == 0 else "vector")()
         nc.vector.tensor_tensor(out=dist_cols[:, :, :CHUNKS], in0=dist_parts[:, 0], in1=dist_parts[:, 1], op=ALU.add)
-        for n in range(NODES):
-            if n >= 2:
-                open_banks.append(new_bank())
-                dx_passes(open_banks[n], n, 0, 0)
-            dx_passes(open_banks[n], n, 0, 1)
-            dx_finish(open_banks[n], n, 0, "vector")
-        quantise_job(tok[1])
-        row_bank = sum_banks[0]
-        for t in range(4):
-            nc.tensor.transpose(row_bank[:, t : BANK : 4], dist_cols[:, t, :], ident[:])
-        row = new_result()
-        nc.scalar.copy(out=row[:32, :], in_=row_bank[:32, :])
-        nc.sync.dma_start(out=out_1[2 * H : 2 * H + 1, :].rearrange("o (c f) -> (o c) f", c=CHUNKS), in_=row[:CHUNKS, :])
-        for n in range(NODES):
-            for k in range(4 * n, 4 * n + 4):
-                dw_block(1, k, "vector" if k % 2 else "scalar")()
+        dw_left = list(range(6, 2 * H // P))
+        for m, (hh, n) in enumerate([(0, 2), (0, 3), (1, 0), (1, 1), (1, 2), (1, 3)]):
             bank = new_bank()
-            dx_passes(bank, n, 1, 0)
-            dx_passes(bank, n, 1, 1)
-            dx_finish(bank, n, 1, "vector" if n % 2 else "scalar")
+            dx_passes(bank, n, hh, 0)
+            dx_passes(bank, n, hh, 1)
+            dx_finish(bank, n, hh, "vector" if len(results_made) % 2 else "scalar")
+            for k in dw_left[:2]:
+                dw_block(1, k, "vector" if len(results_made) % 2 else "scalar")()
+            dw_left = dw_left[2:]
+            if m == 0:
+                row_bank = sum_banks[0]
+                for t in range(4):
+                    nc.tensor.transpose(row_bank[:, t : BANK : 4], dist_cols[:, t, :], ident[:])
+                row = new_result()
+                nc.scalar.copy(out=row[:32, :], in_=row_bank[:32, :])
+                nc.sync.dma_start(
+                    out=out_1[2 * H : 2 * H + 1, :].rearrange("o (c f) -> (o c) f", c=CHUNKS), in_=row[:CHUNKS, :]
+                )

@@ -88,8 +88,8 @@ def tile_graphmessagelayer_pa_v_kernel(
             return work.tile([P, 2 * BANK], F32, name="stage", tag="stage", bufs=4, align_bytes=64)
 
         def quantise(key, values, fmt):
-            codes = work.tile([P, BANK], U32, name="codes", tag="codes", bufs=30, align_bytes=64)
-            scales = work.tile([P, BANK], U8, name="scales", tag="scales", bufs=30, align_bytes=64)
+            codes = work.tile([P, BANK], U32, name="codes", tag="codes", bufs=24, align_bytes=64)
+            scales = work.tile([P, BANK], U8, name="scales", tag="scales", bufs=24, align_bytes=64)
             nc.vector.quantize_mx(out=codes[:].bitcast(fmt), scales=scales[:], in_=values)
             mx[key] = (codes, scales, fmt)
 
@@ -121,46 +121,46 @@ def tile_graphmessagelayer_pa_v_kernel(
                         src = every_second_word(words, 512 * j + 256 * a, v)
                     elif key[0] == "we2":
                         words = loaded[key][:].rearrange("p t m -> p (t m)").bitcast(F32)
-                        src = every_second_word(words, 256 * (2 * a + j), v)
+                        src = every_second_word(words, 256 * (2 * j + a), v)
                     elif key[0] == "we1":
                         words = loaded[key[:3]][:].rearrange("p t m -> p (t m)").bitcast(F32)
                         src = every_second_word(words, 512 * (2 * j + a) + 256 * key[3], v)
                     else:
-                        words = d_feat[key[1]][:].bitcast(F32)
-                        src = every_second_word(words, 256 * (NODES * key[2] + k), j)
+                        words = d_rows[key[1]][:].bitcast(F32)
+                        first_word = 4 * P * (2 * j + a) + 2 * P * key[2] + P * v
+                        src = words[:, first_word : first_word + P]
                     nc.tensor.transpose(bank[:, P * k : P * (k + 1)], src, ident[:])
                 banks.append(bank)
             return {"key": key, "banks": banks, "stage": new_stage()}
 
         def empty(job, j, engine):
             bank, stage = job["banks"][j], job["stage"]
-            if job["key"][0] == "d_tok":
-                out = stage[:, BANK * j : BANK * (j + 1)].bitcast(BF16).rearrange("p (k n) -> p k n", n=NODES)
-                copy(engine, out, bank[:].bitcast(BF16).rearrange("p (n k) -> p k n", n=NODES))
-            elif job["key"][0] == "we2":
-                out = stage[:, BANK * j : BANK * (j + 1)].rearrange("p (r a v) -> p r a v", a=2, v=2)
-                copy(engine, out, bank[:].rearrange("p (a v r) -> p r a v", a=2, v=2))
-            else:
-                out = stage[:, BANK * j : BANK * (j + 1)].rearrange("p (a r v) -> p a r v", a=2, v=2)
-                copy(engine, out, bank[:].rearrange("p (a v r) -> p a r v", a=2, v=2))
+            out = stage[:, BANK * j : BANK * (j + 1)].rearrange("p (a r v) -> p a r v", a=2, v=2)
+            copy(engine, out, bank[:].rearrange("p (a v r) -> p a r v", a=2, v=2))
 
         def quantise_job(job):
-            fmt = E5M2 if job["key"][0] in ("g", "d_tok") else E4M3
+            fmt = E5M2 if job["key"][0] in ("g", "d_tok", "d_feat") else E4M3
             quantise(job["key"], job["stage"][:].bitcast(BF16), fmt)
 
-        def interleave_x(hh):
+        def interleave(key, rows):
             stage = new_stage()
-            dst = stage[:].bitcast(BF16).rearrange("p (c i n) -> p c n i", i=4, n=NODES)
-            src = loaded["x"][:, :, BANK * hh : BANK * (hh + 1)].rearrange("p n (c i) -> p c n i", i=4)
-            nc.vector.tensor_copy(out=dst, in_=src)
-            return {"key": ("x", hh), "stage": stage}
+            dst = stage[:].bitcast(BF16).rearrange("p (c i n) -> p c n i", i=4, n=4)
+            nc.vector.tensor_copy(out=dst, in_=rows.rearrange("p n (c i) -> p c n i", i=4))
+            return {"key": key, "stage": stage}
+
+        def interleave_x(hh):
+            return interleave(("x", hh), loaded["x"][:, :, BANK * hh : BANK * (hh + 1)])
+
+        def interleave_d(c, half):
+            rows = d_rows[c][:].rearrange("p (t k) -> p t k", t=4)[:, :, BANK * half : BANK * (half + 1)]
+            return interleave(("d_feat", c, half), rows)
 
         acts = {}
 
         def activation(i, func, scale):
-            t = work.tile([P, 2, BANK], F32, name="act_t", tag="act_t", bufs=5)
-            src = loaded["pre", i][:].rearrange("q a (w e) -> q e (a w)", e=2)
-            nc.scalar.activation(out=t[:], in_=src, func=func, scale=scale)
+            t = work.tile([P, 4, 2 * P], F32, name="act_t", tag="act_t", bufs=5)
+            src = loaded["pre", i][:].rearrange("q a (w t) -> q (a w) t", t=4)
+            nc.scalar.activation(out=t[:].rearrange("q t w -> q w t"), in_=src, func=func, scale=scale)
             acts[i, func] = t
 
         dh_banks = {}
@@ -176,25 +176,25 @@ def tile_graphmessagelayer_pa_v_kernel(
         dpre = {}
 
         def elementwise(i):
-            part = work.tile([P, 2, 2, BANK // 2], F32, name="part", tag="part", bufs=2)
+            part = work.tile([P, 4, 2 * P], F32, name="part", tag="part", bufs=2)
             for a in range(2):
                 nc.vector.scalar_tensor_tensor(
-                    out=part[:, :, a, :],
-                    in0=acts[i, ACT.Silu][:, :, BANK // 2 * a : BANK // 2 * (a + 1)],
+                    out=part[:, :, P * a : P * (a + 1)],
+                    in0=acts[i, ACT.Silu][:, :, P * a : P * (a + 1)],
                     scalar=1.0,
-                    in1=dh_banks[i, a][:].rearrange("q (e w) -> q e w", e=2),
+                    in1=dh_banks[i, a][:].rearrange("q (t w) -> q t w", t=4),
                     op0=ALU.subtract,
                     op1=ALU.mult,
                 )
             return part
 
         def finish_elementwise(i, part):
-            t = work.tile([P, 2, BANK], F32, name="dpre_t", tag="dpre_t", bufs=3)
+            t = work.tile([P, 4, 2 * P], F32, name="dpre_t", tag="dpre_t", bufs=3)
             nc.vector.scalar_tensor_tensor(
                 out=t[:],
-                in0=acts[i, ACT.Tanh][:].rearrange("q e (w u) -> q u (e w)", u=2),
+                in0=acts[i, ACT.Tanh][:],
                 scalar=1.0,
-                in1=part[:].rearrange("q e a (w u) -> q u (e a w)", u=2),
+                in1=part[:],
                 op0=ALU.add,
                 op1=ALU.mult,
             )
@@ -207,31 +207,25 @@ def tile_graphmessagelayer_pa_v_kernel(
             s = i % STEPS
             for a in range(2):
                 for t in range(4):
-                    u, e = divmod(t, 2)
-                    first_col = 2 * P * e + P * a
                     nc.tensor.matmul(
                         sum_window(i, a)[:, t, :],
-                        lhsT=dpre[i][:, u, first_col : first_col + P],
+                        lhsT=dpre[i][:, t, P * a : P * (a + 1)],
                         rhs=sel[:, 2 * s + a, :],
                         start=True,
                         stop=True,
                     )
 
-        d_feat = {}
+        d_rows = {}
 
-        def empty_sums(i):
+        def empty_sums(i, engines=("vector", "vector")):
             c, s = divmod(i, STEPS)
             if s == 0:
-                d_feat[c] = work.tile([P, 2 * B * NODES * 4], BF16, name="d_feat", tag="d_feat", bufs=2, align_bytes=64)
+                d_rows[c] = work.tile([P, 2 * B * NODES * 4], BF16, name="d_rows", tag="d_rows", bufs=2, align_bytes=64)
             for a in range(2):
                 tl = 2 * s + a
-                sums = sum_window(i, a)[:, :, 2:].rearrange("p t (n b) -> p n b t", b=GRAPHS)
-                out = d_feat[c][:].rearrange("p (n b t) -> p n b t", b=B, t=4)[:, :, GRAPHS * tl : GRAPHS * (tl + 1), :]
-                nc.vector.tensor_copy(out=out, in_=sums)
-
-        def quantise_d_feat(c, half):
-            width = B * NODES * 4
-            quantise(("d_feat", c, half), d_feat[c][:, width * half : width * (half + 1)], E5M2)
+                sums = sum_window(i, a)[:, :, 2:].rearrange("p t (m k) -> p t m k", m=4)
+                out = d_rows[c][:].rearrange("p (t m k) -> p t m k", t=4, m=4)
+                copy(engines[a], out[:, :, :, 2 * GRAPHS * tl : 2 * GRAPHS * (tl + 1)], sums)
 
         results_made = []
 
@@ -250,8 +244,8 @@ def tile_graphmessagelayer_pa_v_kernel(
                 res = new_result()
                 copy(
                     engine,
-                    res[:].rearrange("h (w u e) -> h w u e", u=2, e=2),
-                    bank[:].rearrange("h (u w e) -> h w u e", u=2, e=2),
+                    res[:].rearrange("h (w t) -> h w t", t=4),
+                    bank[:].rearrange("h (t w) -> h w t", t=4),
                 )
                 r0 = H * half + P * hb
                 nc.sync.dma_start(out=out_1[r0 : r0 + P, BANK * c : BANK * (c + 1)], in_=res[:])
@@ -267,7 +261,9 @@ def tile_graphmessagelayer_pa_v_kernel(
         def dx_finish(bank, n, hh, engine):
             res = new_result()
             copy(engine, res[:], bank[:])
-            nc.sync.dma_start(out=out_0[:, n, BANK * hh : BANK * (hh + 1)], in_=res[:])
+            pair, upper = divmod(n, 2)
+            rows = out_0[64 * upper : 64 * (upper + 1), 2 * pair : 2 * pair + 2, BANK * hh : BANK * (hh + 1)]
+            nc.sync.dma_start(out=rows, in_=res[:])
 
         pos = const.tile([P, NODES, 3], BF16, name="pos")
         nc.scalar.dma_start(out=pos[:], in_=positions)
@@ -282,10 +278,10 @@ def tile_graphmessagelayer_pa_v_kernel(
         ident = const.tile([P, P], F32, name="ident")
         make_identity(nc, ident[:])
         warm = const.tile([P, 1], F32, name="warm")
-        nc.scalar.activation(out=warm[:], in_=ident[:, 0:1], func=ACT.Silu, scale=-1.0)
+        nc.scalar.activation(out=warm[:], in_=ident[:, 0:1], func=ACT.Sqrt)
 
         sel = const.tile([P, TILES, SEL_COLS], F32, name="sel")
-        pick = const.tile([P, 2, NODES, GRAPHS], F32, name="pick")
+        pick = const.tile([P, 2, 2, GRAPHS, 2], F32, name="pick")
         in_tile = const.tile([P, TILES], F32, name="in_tile")
         in_place = const.tile([P, GRAPHS], F32, name="in_place")
         dist_parts = const.tile([P, 2, 4, CHUNKS], F32, name="dist_parts")
@@ -294,39 +290,36 @@ def tile_graphmessagelayer_pa_v_kernel(
         nc.vector.memset(sel[:], 0.0)
         nc.vector.memset(dist_cols[:], 0.0)
         pair_view = ident[:].rearrange("q (b i j) -> q b i j", i=NODES, j=NODES)
-        nc.vector.tensor_reduce(out=pick[:, 0], in_=pair_view.rearrange("q b i j -> q i b j"), axis=AXIS.X, op=ALU.add)
-        nc.vector.tensor_reduce(out=pick[:, 1], in_=pair_view.rearrange("q b i j -> q j b i"), axis=AXIS.X, op=ALU.add)
+        nc.vector.tensor_reduce(out=pick[:, 0], in_=pair_view.rearrange("q b (u e) j -> q u b e j", e=2), axis=AXIS.X, op=ALU.add)
+        nc.vector.tensor_reduce(out=pick[:, 1], in_=pair_view.rearrange("q b i (u e) -> q u b e i", e=2), axis=AXIS.X, op=ALU.add)
         graph_view = ident[:].rearrange("b (t g) -> b t g", g=GRAPHS)
         nc.vector.tensor_reduce(out=in_tile[:], in_=graph_view, axis=AXIS.X, op=ALU.add)
         nc.vector.tensor_reduce(out=in_place[:], in_=graph_view.rearrange("b t g -> b g t"), axis=AXIS.X, op=ALU.add)
         nc.vector.tensor_scalar(
             out=sel[:, :, 2:],
-            in0=pick[:].rearrange("q h n g -> q (h n g)").unsqueeze(1).to_broadcast([P, TILES, SUM_COLS]),
+            in0=pick[:].rearrange("q h u g e -> q (h u g e)").unsqueeze(1).to_broadcast([P, TILES, SUM_COLS]),
             scalar1=-0.5,
             scalar2=None,
             op0=ALU.mult,
         )
 
-        half_power = const.tile([P, NODES * NODES], F32, name="half_power")
         rel = const.tile([P, NODES, NODES, 3], F32, name="rel")
         rel_sq = const.tile([P, NODES * NODES, 3], F32, name="rel_sq")
-        sq_xy = const.tile([P, NODES * NODES], F32, name="sq_xy")
         sq = const.tile([P, NODES * NODES], F32, name="sq")
         dist = const.tile([P, NODES * NODES], F32, name="dist")
         dist_spread = const.tile([P, GRAPHS, NODES * NODES], F32, name="dist_spread")
-        nc.gpsimd.memset(half_power[:], 0.5)
-        nc.gpsimd.tensor_tensor(
+        nc.vector.tensor_tensor(
             out=rel[:],
             in0=pos[:].unsqueeze(2).to_broadcast([P, NODES, NODES, 3]),
             in1=pos[:].unsqueeze(1).to_broadcast([P, NODES, NODES, 3]),
             op=ALU.subtract,
         )
         rel_flat = rel[:].rearrange("b i j c -> b (i j) c")
-        nc.gpsimd.tensor_tensor(out=rel_sq[:], in0=rel_flat, in1=rel_flat, op=ALU.mult)
-        nc.gpsimd.tensor_tensor(out=sq_xy[:], in0=rel_sq[:, :, 0], in1=rel_sq[:, :, 1], op=ALU.add)
-        nc.gpsimd.tensor_tensor(out=sq[:], in0=sq_xy[:], in1=rel_sq[:, :, 2], op=ALU.add)
-        nc.gpsimd.tensor_tensor(out=dist[:], in0=sq[:], in1=half_power[:], op=ALU.pow)
-        nc.gpsimd.tensor_tensor(
+        nc.vector.tensor_tensor(out=rel_sq[:], in0=rel_flat, in1=rel_flat, op=ALU.mult)
+        nc.vector.tensor_reduce(out=sq[:], in_=rel_sq[:], axis=AXIS.X, op=ALU.add)
+        nc.scalar.activation(out=dist[:], in_=sq[:], func=ACT.Sqrt)
+        nc.scalar.activation(out=warm[:], in_=ident[:, 0:1], func=ACT.Silu, scale=-1.0)
+        nc.vector.tensor_tensor(
             out=dist_spread[:],
             in0=dist[:].unsqueeze(1).to_broadcast([P, GRAPHS, NODES * NODES]),
             in1=in_place[:].unsqueeze(2).to_broadcast([P, GRAPHS, NODES * NODES]),
@@ -379,13 +372,11 @@ def tile_graphmessagelayer_pa_v_kernel(
                     out=sel[:, :, 0], in0=dist_bank[:, :TILES], scalar1=-0.5, scalar2=None, op0=ALU.mult
                 )
             if i >= 2:
-                empty_sums(i - 2)
+                empty_sums(i - 2, ("vector", "scalar") if False else ("vector", "vector"))
             if i >= 1:
                 finish_elementwise(i - 1, part)
             for job in waiting:
                 quantise_job(job)
-            if i in (10, 11):
-                quantise_d_feat(0, i - 10)
             waiting = [turn(key) for key in turns[i]]
             if i + 1 < last:
                 activation(i + 1, ACT.Silu, -1.0)
@@ -403,6 +394,8 @@ def tile_graphmessagelayer_pa_v_kernel(
             part = elementwise(i)
             if i in (3, 5):
                 waiting.append(interleave_x((3, 5).index(i)))
+            if i in (11, 13):
+                waiting.append(interleave_d(0, (11, 13).index(i)))
             for finish in finishes:
                 finish()
             if i == 0:
@@ -417,49 +410,54 @@ def tile_graphmessagelayer_pa_v_kernel(
             else:
                 node_sums(i - 1)
 
-        empty_sums(last - 2)
-        finish_elementwise(last - 1, part)
         for job in waiting:
             quantise_job(job)
+        finish_elementwise(last - 1, part)
+        empty_sums(last - 2)
         final_we1 = turn(we1_jobs[-1])
         empty(final_we1, 0, "scalar")
-        empty(final_we1, 1, "scalar")
-        for k in dw_left[:6]:
+        empty(final_we1, 1, "vector")
+        for k in dw_left[:2]:
             dw_block(0, k, "scalar")()
         node_sums(last - 1)
-        for k in dw_left[6:]:
+        for k in dw_left[2:]:
             dw_block(0, k, "scalar")()
-        open_banks = []
-        for n in range(2):
-            bank = new_bank()
-            dx_passes(bank, n, 0, 0)
-            open_banks.append(bank)
         empty_sums(last - 1)
-        tok = [turn(("d_tok", 1, half)) for half in range(2)]
-        quantise_d_feat(1, 0)
-        quantise_d_feat(1, 1)
-        empty(tok[0], 0, "scalar")
-        empty(tok[0], 1, "vector")
-        empty(tok[1], 0, "scalar")
-        quantise_job(tok[0])
-        for n in range(2):
-            dx_passes(open_banks[n], n, 0, 1)
-            dx_finish(open_banks[n], n, 0, "scalar")
-        empty(tok[1], 1, "vector")
-        for k in range(0, 3):
-            dw_block(1, k, "scalar")()
-        quantise_job(tok[1])
-        quantise_job(final_we1)
         for a in range(2):
             kept = sum_banks[a][:].rearrange("p (t k) -> p t k", t=4)[:, :, 0 : 2 * last : 2]
             nc.vector.tensor_reduce(
                 out=dist_parts[:, a], in_=kept.rearrange("p t (c k) -> p t c k", c=CHUNKS), axis=AXIS.X, op=ALU.add
             )
-        for k in range(3, 6):
-            dw_block(1, k, "scalar" if k % 2 == 0 else "vector")()
+        tok = [turn(("d_tok", 1, half)) for half in range(2)]
+        empty(tok[0], 0, "scalar")
+        empty(tok[0], 1, "vector")
+        quantise_job(tok[0])
+        empty(tok[1], 0, "scalar")
+        empty(tok[1], 1, "scalar")
+        feat = interleave_d(1, 0)
+        open_banks = list(sum_banks)
+        for n in range(2):
+            dx_passes(open_banks[n], n, 0, 0)
+        for k in range(0, 2):
+            dw_block(1, k, "scalar")()
+        for n in range(2, 4):
+            open_banks.append(new_bank())
+            dx_passes(open_banks[n], n, 0, 0)
         nc.vector.tensor_tensor(out=dist_cols[:, :, :CHUNKS], in0=dist_parts[:, 0], in1=dist_parts[:, 1], op=ALU.add)
-        dw_left = list(range(6, 2 * H // P))
-        for m, (hh, n) in enumerate([(0, 2), (0, 3), (1, 0), (1, 1), (1, 2), (1, 3)]):
+        quantise_job(feat)
+        feat = interleave_d(1, 1)
+        for k in range(2, 6):
+            dw_block(1, k, "scalar")()
+        quantise_job(tok[1])
+        quantise_job(feat)
+        quantise_job(final_we1)
+        for k in range(6, 8):
+            dw_block(1, k, "scalar" if k % 2 else "vector")()
+        for n in range(4):
+            dx_passes(open_banks[n], n, 0, 1)
+            dx_finish(open_banks[n], n, 0, "scalar" if n % 2 else "vector")
+        dw_left = list(range(8, 2 * H // P))
+        for m, (hh, n) in enumerate([(1, 0), (1, 1), (1, 2), (1, 3)]):
             bank = new_bank()
             dx_passes(bank, n, hh, 0)
             dx_passes(bank, n, hh, 1)
@@ -468,7 +466,7 @@ def tile_graphmessagelayer_pa_v_kernel(
                 dw_block(1, k, "vector" if len(results_made) % 2 else "scalar")()
             dw_left = dw_left[2:]
             if m == 0:
-                row_bank = sum_banks[0]
+                row_bank = new_bank()
                 for t in range(4):
                     nc.tensor.transpose(row_bank[:, t : BANK : 4], dist_cols[:, t, :], ident[:])
                 row = new_result()

from contextlib import ExitStack

import concourse.mybir as mybir
from concourse.masks import make_identity

B, NODES, H, F, M = 128, 4, 1024, 1024, 1024
PAIRS = B * NODES * NODES
FLOPS = 2 * PAIRS * M * F + 2 * 2 * B * NODES * 2 * F * H
BYTES = 2 * (B * NODES * H + B * NODES * 3 + 2 * H * F + F * M + PAIRS * M) + 4 * (
    PAIRS * F + B * NODES * H + (2 * H + 1) * F
)

F32 = mybir.dt.float32
BF16 = mybir.dt.bfloat16
U32 = mybir.dt.uint32
U8 = mybir.dt.uint8
E4M3 = mybir.dt.float8_e4m3fn_x4
E5M2 = mybir.dt.float8_e5m2_x4
ACT = mybir.ActivationFunctionType
ALU = mybir.AluOpType
AXIS = mybir.AxisListType

P = 128
BANK = 512
CHUNKS = F // BANK
TILES = PAIRS // P
STEPS = TILES // 2
GRAPHS = P // (NODES * NODES)
SUM_COLS = 2 * GRAPHS * NODES
SEL_COLS = SUM_COLS + 2


def tile_graphmessagelayer_pa_v_kernel(
    tc, node_state, positions, We1, be1, We2, be2, pre, grad_out, out_0, out_1
):
    nc = tc.nc
    g_rows = grad_out.rearrange("b i j m -> (b i j) m")
    pre_rows = pre.rearrange("b i j f -> (b i j) f")

    with ExitStack() as ctx:
        const = ctx.enter_context(tc.tile_pool(name="const", bufs=1))
        work = ctx.enter_context(tc.tile_pool(name="work", bufs=1))
        psum = ctx.enter_context(tc.psum_pool(name="psum", bufs=1))
        ctx.enter_context(tc.manual_schedule())

        def new_bank():
            return psum.tile([P, BANK], F32, name="bank", tag="bank", bufs=6)

        def copy(engine, out, in_):
            if engine == "scalar":
                nc.scalar.copy(out=out, in_=in_)
            else:
                nc.vector.tensor_copy(out=out, in_=in_)

        loaded = {}
        mx = {}

        def load_g(s):
            t = work.tile([P, 2, M], BF16, name="raw4", tag="raw4", bufs=5)
            nc.sync.dma_start(out=t[:], in_=g_rows[2 * P * s : 2 * P * (s + 1), :].rearrange("(t q) m -> q t m", t=2))
            loaded["g", s] = t

        def load_we2(c, g):
            t = work.tile([P, 4, BANK], BF16, name="raw4", tag="raw4", bufs=5)
            rows = We2[BANK * c : BANK * (c + 1), BANK * g : BANK * (g + 1)]
            nc.sync.dma_start(out=t[:], in_=rows.rearrange("(p t) m -> p t m", t=4))
            loaded["we2", c, g] = t

        def load_pre(i):
            c, s = divmod(i, STEPS)
            t = work.tile([P, 2, BANK], F32, name="pre_t", tag="pre_t", bufs=6)
            rows = pre_rows[2 * P * s : 2 * P * (s + 1), BANK * c : BANK * (c + 1)]
            nc.sync.dma_start(out=t[:], in_=rows.rearrange("(t q) f -> q t f", t=2))
            loaded["pre", i] = t

        def load_x():
            t = work.tile([P, NODES, H], BF16, name="raw8", tag="raw8", bufs=3)
            nc.sync.dma_start(out=t[:], in_=node_state)
            loaded["x"] = t

        def load_we1(half, hh):
            t = work.tile([P, 4, F], BF16, name="raw8", tag="raw8", bufs=3)
            r0 = H * half + BANK * hh
            nc.sync.dma_start(out=t[:], in_=We1[r0 : r0 + BANK, :].rearrange("(t p) f -> p t f", t=4))
            loaded["we1", half, hh] = t

        def new_stage():
            return work.tile([P, 2 * BANK], F32, name="stage", tag="stage", bufs=4, align_bytes=64)

        def quantise(key, values, fmt):
            codes = work.tile([P, BANK], U32, name="codes", tag="codes", bufs=24, align_bytes=64)
            scales = work.tile([P, BANK], U8, name="scales", tag="scales", bufs=24, align_bytes=64)
            nc.vector.quantize_mx(out=codes[:].bitcast(fmt), scales=scales[:], in_=values)
            mx[key] = (codes, scales, fmt)

        def matmul_mx(bank, lhs_key, lhs_block, rhs_key, start, stop):
            l_codes, l_scales, l_fmt = mx[lhs_key]
            r_codes, r_scales, r_fmt = mx[rhs_key]
            cols = slice(P * lhs_block, P * (lhs_block + 1))
            nc.tensor.matmul_mx(
                out=bank[:],
                lhsT=l_codes[:, cols].bitcast(l_fmt),
                lhsT_scale=l_scales[:, cols],
                rhs=r_codes[:].bitcast(r_fmt),
                rhs_scale=r_scales[:],
                start=start,
                stop=stop,
            )

        def every_second_word(words, first, v):
            return words[:, first + v : first + 2 * P : 2]

        def turn(key):
            banks = []
            for j in range(2):
                bank = new_bank()
                for k in range(4):
                    a, v = divmod(k, 2)
                    if key[0] == "g":
                        words = loaded[key][:].rearrange("p t m -> p (t m)").bitcast(F32)
                        src = every_second_word(words, 512 * j + 256 * a, v)
                    elif key[0] == "we2":
                        words = loaded[key][:].rearrange("p t m -> p (t m)").bitcast(F32)
                        src = every_second_word(words, 256 * (2 * j + a), v)
                    elif key[0] == "we1":
                        words = loaded[key[:3]][:].rearrange("p t m -> p (t m)").bitcast(F32)
                        src = every_second_word(words, 512 * (2 * j + a) + 256 * key[3], v)
                    else:
                        words = d_rows[key[1]][:].bitcast(F32)
                        first_word = 4 * P * (2 * j + a) + 2 * P * key[2] + P * v
                        src = words[:, first_word : first_word + P]
                    nc.tensor.transpose(bank[:, P * k : P * (k + 1)], src, ident[:])
                banks.append(bank)
            return {"key": key, "banks": banks, "stage": new_stage()}

        def empty(job, j, engine):
            bank, stage = job["banks"][j], job["stage"]
            out = stage[:, BANK * j : BANK * (j + 1)].rearrange("p (a r v) -> p a r v", a=2, v=2)
            copy(engine, out, bank[:].rearrange("p (a v r) -> p a r v", a=2, v=2))

        def quantise_job(job):
            fmt = E5M2 if job["key"][0] in ("g", "d_tok", "d_feat") else E4M3
            quantise(job["key"], job["stage"][:].bitcast(BF16), fmt)

        def interleave(key, rows):
            stage = new_stage()
            dst = stage[:].bitcast(BF16).rearrange("p (c i n) -> p c n i", i=4, n=4)
            nc.vector.tensor_copy(out=dst, in_=rows.rearrange("p n (c i) -> p c n i", i=4))
            return {"key": key, "stage": stage}

        def interleave_x(hh):
            return interleave(("x", hh), loaded["x"][:, :, BANK * hh : BANK * (hh + 1)])

        def interleave_d(c, half):
            rows = d_rows[c][:].rearrange("p (t k) -> p t k", t=4)[:, :, BANK * half : BANK * (half + 1)]
            return interleave(("d_feat", c, half), rows)

        acts = {}

        def activation(i, func, scale):
            t = work.tile([P, 4, 2 * P], F32, name="act_t", tag="act_t", bufs=5)
            src = loaded["pre", i][:].rearrange("q a (w t) -> q (a w) t", t=4)
            nc.scalar.activation(out=t[:].rearrange("q t w -> q w t"), in_=src, func=func, scale=scale)
            acts[i, func] = t

        dh_banks = {}

        def dh_matmuls(i):
            c, s = divmod(i, STEPS)
            for a in range(2):
                bank = new_bank()
                for g in range(2):
                    matmul_mx(bank, ("g", s), 2 * a + g, ("we2", c, g), g == 0, g == 1)
                dh_banks[i, a] = bank

        dpre = {}

        def elementwise(i):
            part = work.tile([P, 4, 2 * P], F32, name="part", tag="part", bufs=2)
            for a in range(2):
                nc.vector.scalar_tensor_tensor(
                    out=part[:, :, P * a : P * (a + 1)],
                    in0=acts[i, ACT.Silu][:, :, P * a : P * (a + 1)],
                    scalar=1.0,
                    in1=dh_banks[i, a][:].rearrange("q (t w) -> q t w", t=4),
                    op0=ALU.subtract,
                    op1=ALU.mult,
                )
            return part

        def finish_elementwise(i, part):
            t = work.tile([P, 4, 2 * P], F32, name="dpre_t", tag="dpre_t", bufs=3)
            nc.vector.scalar_tensor_tensor(
                out=t[:],
                in0=acts[i, ACT.Tanh][:],
                scalar=1.0,
                in1=part[:],
                op0=ALU.add,
                op1=ALU.mult,
            )
            dpre[i] = t

        def sum_window(i, a):
            return sum_banks[a][:].rearrange("p (t k) -> p t k", t=4)[:, :, 2 * i : 2 * i + SEL_COLS]

        def node_sums(i):
            s = i % STEPS
            for a in range(2):
                for t in range(4):
                    nc.tensor.matmul(
                        sum_window(i, a)[:, t, :],
                        lhsT=dpre[i][:, t, P * a : P * (a + 1)],
                        rhs=sel[:, 2 * s + a, :],
                        start=True,
                        stop=True,
                    )

        d_rows = {}

        def empty_sums(i, engines=("vector", "vector")):
            c, s = divmod(i, STEPS)
            if s == 0:
                d_rows[c] = work.tile([P, 2 * B * NODES * 4], BF16, name="d_rows", tag="d_rows", bufs=2, align_bytes=64)
            for a in range(2):
                tl = 2 * s + a
                sums = sum_window(i, a)[:, :, 2:].rearrange("p t (m k) -> p t m k", m=4)
                out = d_rows[c][:].rearrange("p (t m k) -> p t m k", t=4, m=4)
                copy(engines[a], out[:, :, :, 2 * GRAPHS * tl : 2 * GRAPHS * (tl + 1)], sums)

        results_made = []

        def new_result():
            results_made.append(None)
            if len(results_made) > 10 and len(results_made) % 2:
                return work.tile([P, BANK], F32, name="pre_t", tag="pre_t", bufs=6)
            return work.tile([P, BANK], F32, name="result", tag="result", bufs=7)

        def dw_block(c, k, engine):
            half, hb = divmod(k, H // P)
            bank = new_bank()
            matmul_mx(bank, ("x", hb // 4), hb % 4, ("d_tok", c, half), True, True)

            def finish():
                res = new_result()
                copy(
                    engine,
                    res[:].rearrange("h (w t) -> h w t", t=4),
                    bank[:].rearrange("h (t w) -> h w t", t=4),
                )
                r0 = H * half + P * hb
                nc.sync.dma_start(out=out_1[r0 : r0 + P, BANK * c : BANK * (c + 1)], in_=res[:])

            return finish

        def dx_passes(bank, n, hh, c):
            for half in range(2):
                matmul_mx(
                    bank, ("d_feat", c, half), n, ("we1", half, hh, c), c == 0 and half == 0, c == 1 and half == 1
                )

        def dx_finish(bank, n, hh, engine):
            res = new_result()
            copy(engine, res[:], bank[:])
            pair, upper = divmod(n, 2)
            rows = out_0[64 * upper : 64 * (upper + 1), 2 * pair : 2 * pair + 2, BANK * hh : BANK * (hh + 1)]
            nc.sync.dma_start(out=rows, in_=res[:])

        pos = const.tile([P, NODES, 3], BF16, name="pos")
        nc.scalar.dma_start(out=pos[:], in_=positions)
        load_we2(0, 0)
        load_g(0)
        load_we2(0, 1)
        load_g(1)
        load_pre(0)
        load_g(2)
        load_pre(1)

        ident = const.tile([P, P], F32, name="ident")
        make_identity(nc, ident[:])
        warm = const.tile([P, 1], F32, name="warm")
        nc.scalar.activation(out=warm[:], in_=ident[:, 0:1], func=ACT.Sqrt)

        sel = const.tile([P, TILES, SEL_COLS], F32, name="sel")
        pick = const.tile([P, 2, 2, GRAPHS, 2], F32, name="pick")
        in_tile = const.tile([P, TILES], F32, name="in_tile")
        in_place = const.tile([P, GRAPHS], F32, name="in_place")
        dist_parts = const.tile([P, 2, 4, CHUNKS], F32, name="dist_parts")
        sum_banks = [psum.tile([P, BANK], F32, name="sums", tag="sums", bufs=2) for a in range(2)]
        dist_cols = const.tile([P, 4, P], F32, name="dist_cols")
        nc.vector.memset(sel[:], 0.0)
        nc.vector.memset(dist_cols[:], 0.0)
        pair_view = ident[:].rearrange("q (b i j) -> q b i j", i=NODES, j=NODES)
        nc.vector.tensor_reduce(out=pick[:, 0], in_=pair_view.rearrange("q b (u e) j -> q u b e j", e=2), axis=AXIS.X, op=ALU.add)
        nc.vector.tensor_reduce(out=pick[:, 1], in_=pair_view.rearrange("q b i (u e) -> q u b e i", e=2), axis=AXIS.X, op=ALU.add)
        graph_view = ident[:].rearrange("b (t g) -> b t g", g=GRAPHS)
        nc.vector.tensor_reduce(out=in_tile[:], in_=graph_view, axis=AXIS.X, op=ALU.add)
        nc.vector.tensor_reduce(out=in_place[:], in_=graph_view.rearrange("b t g -> b g t"), axis=AXIS.X, op=ALU.add)
        nc.vector.tensor_scalar(
            out=sel[:, :, 2:],
            in0=pick[:].rearrange("q h u g e -> q (h u g e)").unsqueeze(1).to_broadcast([P, TILES, SUM_COLS]),
            scalar1=-0.5,
            scalar2=None,
            op0=ALU.mult,
        )

        rel = const.tile([P, NODES, NODES, 3], F32, name="rel")
        rel_sq = const.tile([P, NODES * NODES, 3], F32, name="rel_sq")
        sq = const.tile([P, NODES * NODES], F32, name="sq")
        dist = const.tile([P, NODES * NODES], F32, name="dist")
        dist_spread = const.tile([P, GRAPHS, NODES * NODES], F32, name="dist_spread")
        nc.vector.tensor_tensor(
            out=rel[:],
            in0=pos[:].unsqueeze(2).to_broadcast([P, NODES, NODES, 3]),
            in1=pos[:].unsqueeze(1).to_broadcast([P, NODES, NODES, 3]),
            op=ALU.subtract,
        )
        rel_flat = rel[:].rearrange("b i j c -> b (i j) c")
        nc.vector.tensor_tensor(out=rel_sq[:], in0=rel_flat, in1=rel_flat, op=ALU.mult)
        nc.vector.tensor_reduce(out=sq[:], in_=rel_sq[:], axis=AXIS.X, op=ALU.add)
        nc.scalar.activation(out=dist[:], in_=sq[:], func=ACT.Sqrt)
        nc.scalar.activation(out=warm[:], in_=ident[:, 0:1], func=ACT.Silu, scale=-1.0)
        nc.vector.tensor_tensor(
            out=dist_spread[:],
            in0=dist[:].unsqueeze(1).to_broadcast([P, GRAPHS, NODES * NODES]),
            in1=in_place[:].unsqueeze(2).to_broadcast([P, GRAPHS, NODES * NODES]),
            op=ALU.mult,
        )

        first = []
        for key in (("we2", 0, 0), ("g", 0), ("we2", 0, 1)):
            job = turn(key)
            empty(job, 0, "vector")
            empty(job, 1, "scalar")
            if first:
                quantise_job(first[-1])
            first.append(job)
        job = turn(("g", 1))
        empty(job, 0, "vector")
        quantise_job(first[-1])
        empty(job, 1, "vector")
        activation(0, ACT.Silu, -1.0)
        activation(0, ACT.Tanh, 0.5)
        waiting = [job]

        we1_order = [(half, hh) for hh in range(2) for half in range(2)]
        we1_jobs = [("we1", half, hh, c) for half, hh in we1_order for c in range(CHUNKS)]
        turns = {i: [("g", i + 2)] for i in range(STEPS - 2)}
        turns[6] = [("we2", 1, 0), ("we2", 1, 1)]
        turns[10] = [("d_tok", 0, 0)]
        turns[11] = [("d_tok", 0, 1)]
        for i, key in zip([k for k in range(7, 16) if k not in turns], we1_jobs):
            turns[i] = [key]
        dw_left = list(range(2 * H // P))
        last = CHUNKS * STEPS
        we1_steps = (4, 6, 10, 11)

        for i in range(last):
            if i + 3 < STEPS:
                load_g(i + 3)
            if i in (3, 4):
                load_we2(1, i - 3)
            for k in range(i + 2, min(i + 2 + 4, last)):
                if ("pre", k) not in loaded and (k <= 2 * i + 2):
                    load_pre(k)
            if i == 2:
                load_x()
            if i in we1_steps:
                load_we1(*we1_order[we1_steps.index(i)])

            if i == 1:
                nc.vector.tensor_scalar(
                    out=sel[:, :, 0], in0=dist_bank[:, :TILES], scalar1=-0.5, scalar2=None, op0=ALU.mult
                )
            if i >= 2:
                empty_sums(i - 2, ("vector", "scalar") if False else ("vector", "vector"))
            if i >= 1:
                finish_elementwise(i - 1, part)
            for job in waiting:
                quantise_job(job)
            waiting = [turn(key) for key in turns[i]]
            if i + 1 < last:
                activation(i + 1, ACT.Silu, -1.0)
            for job in waiting:
                empty(job, 0, "scalar")
                empty(job, 1, "scalar")
            if i + 1 < last:
                activation(i + 1, ACT.Tanh, 0.5)
            dh_matmuls(i)
            finishes = []
            if i >= 11:
                for k in dw_left[:2]:
                    finishes.append(dw_block(0, k, "scalar"))
                dw_left = dw_left[2:]
            part = elementwise(i)
            if i in (3, 5):
                waiting.append(interleave_x((3, 5).index(i)))
            if i in (11, 13):
                waiting.append(interleave_d(0, (11, 13).index(i)))
            for finish in finishes:
                finish()
            if i == 0:
                dist_bank = new_bank()
                nc.tensor.matmul(
                    dist_bank[:, :TILES],
                    lhsT=dist_spread[:].rearrange("b g k -> b (g k)"),
                    rhs=in_tile[:],
                    start=True,
                    stop=True,
                )
            else:
                node_sums(i - 1)

        for job in waiting:
            quantise_job(job)
        finish_elementwise(last - 1, part)
        empty_sums(last - 2)
        final_we1 = turn(we1_jobs[-1])
        empty(final_we1, 0, "scalar")
        empty(final_we1, 1, "vector")
        for k in dw_left[:2]:
            dw_block(0, k, "scalar")()
        node_sums(last - 1)
        for k in dw_left[2:]:
            dw_block(0, k, "scalar")()
        empty_sums(last - 1)
        for a in range(2):
            kept = sum_banks[a][:].rearrange("p (t k) -> p t k", t=4)[:, :, 0 : 2 * last : 2]
            nc.vector.tensor_reduce(
                out=dist_parts[:, a], in_=kept.rearrange("p t (c k) -> p t c k", c=CHUNKS), axis=AXIS.X, op=ALU.add
            )
        tok = [turn(("d_tok", 1, half)) for half in range(2)]
        empty(tok[0], 0, "scalar")
        empty(tok[0], 1, "vector")
        quantise_job(tok[0])
        empty(tok[1], 0, "scalar")
        empty(tok[1], 1, "scalar")
        feat = interleave_d(1, 0)
        open_banks = list(sum_banks)
        for n in range(2):
            dx_passes(open_banks[n], n, 0, 0)
        for k in range(0, 2):
            dw_block(1, k, "scalar")()
        for n in range(2, 4):
            open_banks.append(new_bank())
            dx_passes(open_banks[n], n, 0, 0)
        nc.vector.tensor_tensor(out=dist_cols[:, :, :CHUNKS], in0=dist_parts[:, 0], in1=dist_parts[:, 1], op=ALU.add)
        quantise_job(feat)
        feat = interleave_d(1, 1)
        for k in range(2, 6):
            dw_block(1, k, "scalar")()
        quantise_job(tok[1])
        quantise_job(feat)
        quantise_job(final_we1)
        for k in range(6, 8):
            dw_block(1, k, "scalar" if k % 2 else "vector")()
        for n in range(4):
            dx_passes(open_banks[n], n, 0, 1)
            dx_finish(open_banks[n], n, 0, "scalar" if n % 2 else "vector")
        dw_left = list(range(8, 2 * H // P))
        for m, (hh, n) in enumerate([(1, 0), (1, 1), (1, 2), (1, 3)]):
            bank = new_bank()
            dx_passes(bank, n, hh, 0)
            dx_passes(bank, n, hh, 1)
            dx_finish(bank, n, hh, "vector" if len(results_made) % 2 else "scalar")
            for k in dw_left[:2]:
                dw_block(1, k, "vector" if len(results_made) % 2 else "scalar")()
            dw_left = dw_left[2:]
            if m == 0:
                row_bank = new_bank()
                for t in range(4):
                    nc.tensor.transpose(row_bank[:, t : BANK : 4], dist_cols[:, t, :], ident[:])
                row = new_result()
                nc.scalar.copy(out=row[:32, :], in_=row_bank[:32, :])
                nc.sync.dma_start(
                    out=out_1[2 * H : 2 * H + 1, :].rearrange("o (c f) -> (o c) f", c=CHUNKS), in_=row[:CHUNKS, :]
                )
